import numpy as np
import ml_dtypes


def mxq(x, axis, fmt="e4m3"):
    dtype, down = {"e4m3": (ml_dtypes.float8_e4m3fn, 7), "e5m2": (ml_dtypes.float8_e5m2, 14)}[fmt]
    v = np.moveaxis(np.asarray(x, np.float32).astype(ml_dtypes.bfloat16).astype(np.float64), axis, -1)
    blocks = v.reshape(v.shape[:-1] + (-1, 32))
    amax = np.abs(blocks).max(-1, keepdims=True)
    byte = np.maximum(np.where(amax > 0, np.frexp(amax)[1] - 1 + 127, 0) - down, 1)
    scale = np.exp2(byte - 127.0)
    codes = (blocks / scale).astype(np.float32).astype(dtype).astype(np.float64)
    return np.moveaxis((codes * scale).reshape(v.shape), -1, axis)


WIDE = False


def mx_kscale(k):
    if not WIDE:
        return np.ones(k)
    levels = np.array([10, -10, 5, -5, 0])
    if k % 512:
        return np.exp2(np.random.permutation(np.resize(levels, k // 32))).repeat(32)
    a = np.empty((k // 512, 16))
    for p in range(k // 512):
        a[p, :8] = np.random.permutation(np.resize(levels, 8))
        for g in range(8):
            far = levels[np.abs(levels - a[p, g]) >= 10]
            a[p, g + 8] = far[np.random.randint(len(far))]
    return np.exp2(a.ravel()).repeat(32)


BF16 = ml_dtypes.bfloat16


def bf(x):
    return np.asarray(x, np.float32).astype(BF16)


def f64(x):
    return np.asarray(x).astype(np.float64)


B, T, D, H = 8, 128, 1024, 1024


def sigmoid(v):
    return 1.0 / (1.0 + np.exp(-v))


def draw0():
    s = mx_kscale(D)
    return {"x": bf(np.random.standard_normal((B, T, D)) * s),
            "Wq": bf(np.random.standard_normal((H, D)) * 1.0 / np.sqrt(D) / s),
            "bq": bf(np.random.standard_normal(H) * 0.5),
            "Wk": bf(np.random.standard_normal((H, D)) * 0.6 / np.sqrt(D) / s),
            "bk": bf(np.random.standard_normal(H) * 0.3),
            "Wv": bf(np.random.standard_normal((H, D)) * 2.0 / np.sqrt(D) / s),
            "bv": bf(np.random.standard_normal(H) * 0.5),
            "wbias": bf(np.random.uniform(0.0, 1.0, H))}


def core(x, Wq, bq, Wk, bk, Wv, bv, wbias):
    xq = mxq(f64(x), 2, "e4m3")
    Q = (xq @ mxq(f64(Wq), 1, "e4m3").T) + f64(bq)
    K = (xq @ mxq(f64(Wk), 1, "e4m3").T) + f64(bk)
    V = (xq @ mxq(f64(Wv), 1, "e4m3").T) + f64(bv)
    Q_sig = sigmoid(Q)
    numer = np.exp(K + f64(wbias))
    denom = numer.sum(axis=0)
    weighted = (numer * V).sum(axis=0) / denom
    Yt = Q_sig * weighted
    return Yt


def e4m3fn_bytes(y):
    return np.clip(np.asarray(y, np.float64), -448.0, 448.0).astype(np.float32).astype(ml_dtypes.float8_e4m3fn).view(np.uint8)


def e4m3fn_values(b):
    return np.asarray(b, np.uint8).view(ml_dtypes.float8_e4m3fn).astype(np.float64)


def setup_inputs():
    d = draw0()
    x0 = np.asarray(d['x']).astype(np.float64)
    s = (np.max(np.abs(x0), axis=(0, 1), keepdims=True) / 448.0).astype(np.float32)
    out = {}
    for k, v in d.items():
        if k == 'x':
            out['x_bytes'] = e4m3fn_bytes(x0 / s.astype(np.float64))
            out['x_scale'] = s
        else:
            out[k] = v
    return out


def reference(x_bytes, x_scale, Wq, bq, Wk, bk, Wv, bv, wbias):
    return core(e4m3fn_values(x_bytes) * x_scale.astype(np.float64), Wq, bq, Wk, bk, Wv, bv, wbias)

@@ -1,0 +1,354 @@
+from contextlib import ExitStack
+
+import concourse.mybir as mybir
+from concourse.masks import make_identity
+
+FLOPS = 2 * 3 * 1024 * 1024 * 1024
+
+F32 = mybir.dt.float32
+BF16 = mybir.dt.bfloat16
+U32 = mybir.dt.uint32
+U8 = mybir.dt.uint8
+FP8 = mybir.dt.float8_e4m3fn
+FP8X4 = mybir.dt.float8_e4m3fn_x4
+ALU = mybir.AluOpType
+ACT = mybir.ActivationFunctionType
+
+P = 128
+B = 8
+D = 1024
+H = 1024
+NJ = H // P
+CH = 512
+NC = 2
+NG = 2
+
+WFIRST = 4
+LAG = 2
+
+
+def tile_aftattention_kernel(tc, x_bytes, x_scale, Wq, bq, Wk, bk, Wv, bv, wbias, out):
+    nc = tc.nc
+    with ExitStack() as ctx:
+        const = ctx.enter_context(tc.tile_pool(name="const", bufs=1))
+        keep = ctx.enter_context(tc.tile_pool(name="keep", bufs=1))
+        work = ctx.enter_context(tc.tile_pool(name="work", bufs=2))
+        psum = ctx.enter_context(tc.psum_pool(name="psum", bufs=2))
+        ctx.enter_context(tc.manual_schedule())
+
+        xs_bc = const.tile([P, D], F32, name="xs_bc")
+        nc.scalar.dma_start(out=xs_bc[:], in_=x_scale.rearrange("a b k -> (a b k)").partition_broadcast(P))
+
+        brow = const.tile([P, P], BF16, name="brow")
+        nc.gpsimd.memset(brow[:], 0.0)
+        for v, vec in enumerate((bk, wbias, bv, bq)):
+            nc.scalar.dma_start(out=brow[NJ * v : NJ * (v + 1), :], in_=vec.rearrange("(c p) -> c p", p=P))
+
+        x_view = x_bytes.rearrange("b t k -> t b k")
+        xby = []
+        w_dram = {"k": Wk, "v": Wv, "q": Wq}
+        w_raw = {}
+        w_units = [(w, j) for j in range(NJ) for w in ("k", "v", "q")]
+
+        def load_x(q):
+            t = keep.tile([P, 2, D], U8, name="x_bytes_sb%d" % q)
+            nc.sync.dma_start(out=t[:], in_=x_view[:, 2 * q : 2 * q + 2, :])
+            xby.append(t)
+
+        def load_w(w, j):
+            t = keep.tile([P, D], BF16, name="wraw_%s%d" % (w, j))
+            nc.sync.dma_start(out=t[:], in_=w_dram[w][j * P : (j + 1) * P, :])
+            w_raw[(w, j)] = t
+
+        load_x(0)
+        load_x(1)
+        for unit in w_units[:WFIRST]:
+            load_w(*unit)
+        load_x(2)
+        load_x(3)
+        for unit in w_units[WFIRST:]:
+            load_w(*unit)
+
+        warm = const.tile([P, 1], F32, name="warm")
+        nc.gpsimd.memset(warm[:], 0.0)
+        ident = const.tile([P, P], F32, name="ident")
+        make_identity(nc, ident[:])
+        warm2 = const.tile([P, 1], F32, name="warm2")
+        nc.scalar.activation(out=warm2[:], in_=warm[:], func=ACT.Exp)
+
+        bcol = const.tile([P, 4 * NJ], F32, name="bcol")
+        eb = const.tile([P, NJ], F32, name="eb")
+        bvf = bcol[:, 2 * NJ : 3 * NJ]
+        hbq = const.tile([P, NJ], F32, name="hbq")
+        brow32 = const.tile([P, P], F32, name="brow32")
+        nc.gpsimd.tensor_copy(out=brow32[:], in_=brow[:])
+
+        def bias_columns():
+            bps = psum.tile([P, P], F32, name="bps", tag="sd", bufs=4)
+            nc.tensor.transpose(bps[:], brow32[:], ident[:])
+            nc.scalar.copy(out=bcol[:], in_=bps[:, 0 : 4 * NJ])
+            nc.gpsimd.tensor_tensor(out=eb[:], in0=bcol[:, 0:NJ], in1=bcol[:, NJ : 2 * NJ], op=ALU.add)
+            nc.gpsimd.tensor_scalar(
+                out=hbq[:], in0=bcol[:, 3 * NJ : 4 * NJ], scalar1=0.5, scalar2=0.0, op0=ALU.mult, op1=ALU.add
+            )
+
+        xc = {}
+        xsc = {}
+        for g in range(NG):
+            for c in range(NC):
+                xc[(g, c)] = keep.tile([P, CH], U32, name="xc_%d_%d" % (g, c), align_bytes=64)
+                xsc[(g, c)] = keep.tile([P, CH], U8, name="xsc_%d_%d" % (g, c), align_bytes=64)
+        wc = {}
+        wsc = {}
+        grps = {}
+
+        def turn(key, sources):
+            bank = psum.tile([P, 512], F32, name="bank", tag="sd", bufs=4)
+            for n, src in enumerate(sources):
+                nc.tensor.transpose(bank[:, n * P : (n + 1) * P], src, ident[:])
+            grp = work.tile([P, 1024], BF16, name="grp", tag="grp", bufs=8, align_bytes=64)
+            nc.scalar.copy(
+                out=grp[:].bitcast(F32).rearrange("p (i r u) -> p i r u", i=2, u=2),
+                in_=bank[:].rearrange("p (i u r) -> p i r u", i=2, u=2),
+            )
+            grps[key] = grp
+
+        def every_second(words, g, u):
+            return words[:, 256 * g + u : 256 * (g + 1) : 2]
+
+        def w_turn(w, j):
+            words = w_raw[(w, j)][:].bitcast(F32)
+            turn((w, j), [every_second(words, g, u) for g in range(NG) for u in range(2)])
+
+        def w_quant(w, j):
+            c_t = keep.tile([P, 256], U32, name="wc_%s%d" % (w, j), align_bytes=64)
+            s_t = keep.tile([P, 256], U8, name="wsc_%s%d" % (w, j), align_bytes=64)
+            wc[(w, j)] = c_t
+            wsc[(w, j)] = s_t
+            nc.vector.quantize_mx(out=c_t[:].bitcast(FP8X4), scales=s_t[:], in_=grps[(w, j)][:])
+
+        xb = {}
+
+        def widen(b):
+            t = work.tile([P, D], BF16, name="xb", tag="xb", bufs=4)
+            nc.vector.tensor_tensor(out=t[:], in0=xby[b // 2][:, b % 2, :].bitcast(FP8), in1=xs_bc[:], op=ALU.mult)
+            xb[b] = t
+
+        def x_turn(q, g):
+            turn(("x", q, g), [every_second(xb[2 * q + i][:].bitcast(F32), g, u) for i in range(2) for u in range(2)])
+
+        def x_quant(q, g):
+            c = q // 2
+            cols = slice((q % 2) * 256, (q % 2) * 256 + 256)
+            nc.vector.quantize_mx(
+                out=xc[(g, c)][:, cols].bitcast(FP8X4), scales=xsc[(g, c)][:, cols], in_=grps[("x", q, g)][:]
+            )
+
+        def project(w, j, c, tag, bufs):
+            acc = psum.tile([P, CH], F32, name="acc", tag=tag, bufs=bufs)
+            for g in range(NG):
+                gs = slice(g * P, (g + 1) * P)
+                nc.tensor.matmul_mx(
+                    out=acc[:],
+                    lhsT=wc[(w, j)][:, gs].bitcast(FP8X4),
+                    lhsT_scale=wsc[(w, j)][:, gs],
+                    rhs=xc[(g, c)][:].bitcast(FP8X4),
+                    rhs_scale=xsc[(g, c)][:],
+                    start=(g == 0),
+                    stop=(g == NG - 1),
+                )
+            return acc
+
+        out_view = out.rearrange("b t h -> t b h")
+        ees = {}
+        ths = {}
+        vpss = {}
+        part = {}
+        tots = {}
+        whs = {}
+        whts = {}
+        thts = {}
+
+        def kproj(j, c):
+            ees[(j, c)] = work.tile([P, 2, CH], F32, name="ee", tag="ee", bufs=4)
+            kps = project("k", j, c, "sd", 4)
+            nc.scalar.activation(out=ees[(j, c)][:, 0, :], in_=kps[:], func=ACT.Exp, bias=eb[:, j : j + 1], scale=1.0)
+
+        def vproj(j, c):
+            vpss[(j, c)] = project("v", j, c, "v", 2)
+
+        def qproj(j, c):
+            if c == 0:
+                ths[j] = work.tile([P, B * P], F32, name="th", tag="th", bufs=LAG + 3)
+            qps = project("q", j, c, "sd", 4)
+            nc.scalar.activation(
+                out=ths[j][:, c * CH : (c + 1) * CH], in_=qps[:], func=ACT.Tanh, bias=hbq[:, j : j + 1], scale=0.5
+            )
+
+        def ev(j, c):
+            nc.vector.scalar_tensor_tensor(
+                out=ees[(j, c)][:, 1, :],
+                in0=vpss[(j, c)][:],
+                scalar=bvf[:, j : j + 1],
+                in1=ees[(j, c)][:, 0, :],
+                op0=ALU.add,
+                op1=ALU.mult,
+            )
+
+        a1s = {}
+
+        def t1(j, c, eng):
+            ee = ees[(j, c)]
+            a1s[(j, c)] = work.tile([P, 2, 256], F32, name="a1", tag="a1", bufs=3)
+            eng.tensor_tensor(out=a1s[(j, c)][:], in0=ee[:, :, 0:256], in1=ee[:, :, 256:512], op=ALU.add)
+
+        def t2(j, c, eng):
+            a1 = a1s[(j, c)]
+            if c == 0:
+                a2 = work.tile([P, 2, P], F32, name="a2c0", tag="a2c0", bufs=LAG + 3)
+            else:
+                a2 = work.tile([P, 2, P], F32, name="a2c1", tag="a2c1")
+            eng.tensor_tensor(out=a2[:], in0=a1[:, :, 0:P], in1=a1[:, :, P : 2 * P], op=ALU.add)
+            part[(j, c)] = a2
+
+        def t3(j, eng):
+            s3 = work.tile([P, 2, P], F32, name="s3", tag="s3")
+            eng.tensor_tensor(out=s3[:], in0=part[(j, 1)][:], in1=part[(j, 0)][:], op=ALU.add)
+            tots[j] = s3
+
+        rdens = {}
+
+        def recip(j):
+            rdens[j] = work.tile([P, P], F32, name="rden", tag="rden")
+            nc.vector.reciprocal(out=rdens[j][:], in_=tots[j][:, 0, :])
+
+        def whmul(j):
+            wh = work.tile([P, P], F32, name="wh", tag="wh")
+            nc.vector.scalar_tensor_tensor(
+                out=wh[:], in0=tots[j][:, 1, :], scalar=0.5, in1=rdens[j][:], op0=ALU.mult, op1=ALU.mult
+            )
+            whs[j] = wh
+
+        def back_w(j):
+            wtp = psum.tile([P, P], F32, name="wtp", tag="sd", bufs=4)
+            nc.tensor.transpose(wtp[:], whs[j][:], ident[:])
+            wht = work.tile([P, P], F32, name="wht", tag="wht")
+            nc.scalar.copy(out=wht[:], in_=wtp[:])
+            whts[j] = wht
+
+        def back_th(j, c):
+            if True:
+                tht = psum.tile([P, 512], F32, name="tht", tag="tht", bufs=2)
+                for i in range(4):
+                    b = 4 * c + i
+                    nc.tensor.transpose(tht[:, i * P : (i + 1) * P], ths[j][:, b * P : (b + 1) * P], ident[:])
+                thts[(j, c)] = tht
+
+        outs = {}
+
+        def fin(j, c):
+            if c == 0:
+                outs[j] = work.tile([P, B, P], F32, name="o", tag="o", bufs=3)
+            o = outs[j]
+            if True:
+                bs = slice(4 * c, 4 * c + 4)
+                nc.vector.scalar_tensor_tensor(
+                    out=o[:, bs, :],
+                    in0=thts[(j, c)][:].rearrange("p (b h) -> p b h", b=4),
+                    scalar=1.0,
+                    in1=whts[j][:].unsqueeze(1).to_broadcast([P, 4, P]),
+                    op0=ALU.add,
+                    op1=ALU.mult,
+                )
+                nc.sync.dma_start(out=out_view[:, bs, j * P : (j + 1) * P], in_=o[:, bs, :])
+
+        pos = [0, 0]
+
+        def w_next():
+            if pos[0] < len(w_units):
+                w_turn(*w_units[pos[0]])
+                pos[0] = pos[0] + 1
+
+        def w_quant_turned(limit=99):
+            for i in range(pos[1], min(pos[0], pos[1] + limit)):
+                w_quant(*w_units[i])
+                pos[1] = i + 1
+
+        gp = nc.gpsimd
+        ve = nc.vector
+        widen(0)
+        widen(1)
+        w_next()
+        w_next()
+        x_turn(0, 0)
+        x_turn(0, 1)
+        widen(2)
+        widen(3)
+        w_next()
+        bias_columns()
+        x_turn(1, 0)
+        x_turn(1, 1)
+        w_next()
+        w_next()
+        w_quant_turned(2)
+        x_quant(0, 0)
+        x_quant(0, 1)
+        w_quant_turned(1)
+        x_quant(1, 0)
+        x_quant(1, 1)
+        w_quant_turned()
+        w_next()
+        V0 = (7,)
+        V1 = (7,)
+        for n in range(NJ + LAG + 1):
+            a = n
+            b = n - LAG
+            r = b - 1
+            if a < NJ:
+                kproj(a, 0)
+                vproj(a, 0)
+                qproj(a, 0)
+            if 0 <= b < NJ:
+                kproj(b, 1)
+                vproj(b, 1)
+                qproj(b, 1)
+            if n < 2:
+                widen(4 + 2 * n)
+                widen(5 + 2 * n)
+            if n == 0:
+                w_quant_turned()
+            if a < NJ:
+                ev(a, 0)
+                e0 = ve if a in V0 else gp
+                t1(a, 0, e0)
+                t2(a, 0, e0)
+            if 0 <= b < NJ:
+                ev(b, 1)
+            if 0 <= r < NJ and r not in V1:
+                recip(r)
+                whmul(r)
+            if 0 <= b < NJ:
+                e1 = ve if b in V1 else gp
+                t1(b, 1, e1)
+                t2(b, 1, e1)
+                t3(b, e1)
+                if b in V1:
+                    recip(b)
+                    whmul(b)
+            w_next()
+            w_next()
+            w_next()
+            if n < 2:
+                x_turn(2 + n, 0)
+                x_turn(2 + n, 1)
+            if 0 <= r < NJ:
+                back_th(r, 0)
+                back_th(r, 1)
+                back_w(r)
+            w_quant_turned()
+            if n < 2:
+                x_quant(2 + n, 0)
+                x_quant(2 + n, 1)
+            if 0 <= r < NJ:
+                fin(r, 0)
+                fin(r, 1)

@@ -165,7 +165,6 @@ def tile_aftattention_kernel(tc, x_bytes, x_scale, Wq, bq, Wk, bk, Wv, bv, wbias
         vpss = {}
         part = {}
         tots = {}
-        whs = {}
         whts = {}
         thts = {}
 
@@ -211,29 +210,31 @@ def tile_aftattention_kernel(tc, x_bytes, x_scale, Wq, bq, Wk, bk, Wv, bv, wbias
             eng.tensor_tensor(out=a2[:], in0=a1[:, :, 0:P], in1=a1[:, :, P : 2 * P], op=ALU.add)
             part[(j, c)] = a2
 
-        def t3(j, eng):
-            s3 = work.tile([P, 2, P], F32, name="s3", tag="s3")
-            eng.tensor_tensor(out=s3[:], in0=part[(j, 1)][:], in1=part[(j, 0)][:], op=ALU.add)
-            tots[j] = s3
-
         rdens = {}
+
+        def back_sums(j):
+            dn = psum.tile([P, 2, P], F32, name="dn", tag="sd", bufs=4)
+            for s in range(2):
+                for c in range(NC):
+                    nc.tensor.matmul(
+                        out=dn[:, s, :],
+                        lhsT=part[(j, c)][:, s, :],
+                        rhs=ident[:],
+                        is_transpose=True,
+                        start=(c == 0),
+                        stop=(c == NC - 1),
+                    )
+            tots[j] = dn
 
         def recip(j):
             rdens[j] = work.tile([P, P], F32, name="rden", tag="rden")
             nc.vector.reciprocal(out=rdens[j][:], in_=tots[j][:, 0, :])
 
         def whmul(j):
-            wh = work.tile([P, P], F32, name="wh", tag="wh")
-            nc.vector.scalar_tensor_tensor(
-                out=wh[:], in0=tots[j][:, 1, :], scalar=0.5, in1=rdens[j][:], op0=ALU.mult, op1=ALU.mult
-            )
-            whs[j] = wh
-
-        def back_w(j):
-            wtp = psum.tile([P, P], F32, name="wtp", tag="sd", bufs=4)
-            nc.tensor.transpose(wtp[:], whs[j][:], ident[:])
             wht = work.tile([P, P], F32, name="wht", tag="wht")
-            nc.scalar.copy(out=wht[:], in_=wtp[:])
+            nc.vector.scalar_tensor_tensor(
+                out=wht[:], in0=tots[j][:, 1, :], scalar=0.5, in1=rdens[j][:], op0=ALU.mult, op1=ALU.mult
+            )
             whts[j] = wht
 
         def back_th(j, c):
@@ -324,17 +325,12 @@ def tile_aftattention_kernel(tc, x_bytes, x_scale, Wq, bq, Wk, bk, Wv, bv, wbias
                 t2(a, 0, e0)
             if 0 <= b < NJ:
                 ev(b, 1)
-            if 0 <= r < NJ and r not in V1:
-                recip(r)
-                whmul(r)
             if 0 <= b < NJ:
                 e1 = ve if b in V1 else gp
                 t1(b, 1, e1)
                 t2(b, 1, e1)
-                t3(b, e1)
-                if b in V1:
-                    recip(b)
-                    whmul(b)
+            if 0 <= r < NJ:
+                back_sums(r)
             w_next()
             w_next()
             w_next()
@@ -344,7 +340,8 @@ def tile_aftattention_kernel(tc, x_bytes, x_scale, Wq, bq, Wk, bk, Wv, bv, wbias
             if 0 <= r < NJ:
                 back_th(r, 0)
                 back_th(r, 1)
-                back_w(r)
+                recip(r)
+                whmul(r)
             w_quant_turned()
             if n < 2:
                 x_quant(2 + n, 0)

@@ -23,8 +23,10 @@ CH = 512
 NC = 2
 NG = 2
 
-WFIRST = 4
 LAG = 2
+WFIRST = 4
+TSUM_FROM = 6
+VSUM_FROM = 7
 
 
 def tile_aftattention_kernel(tc, x_bytes, x_scale, Wq, bq, Wk, bk, Wv, bv, wbias, out):
@@ -35,6 +37,8 @@ def tile_aftattention_kernel(tc, x_bytes, x_scale, Wq, bq, Wk, bk, Wv, bv, wbias
         work = ctx.enter_context(tc.tile_pool(name="work", bufs=2))
         psum = ctx.enter_context(tc.psum_pool(name="psum", bufs=2))
         ctx.enter_context(tc.manual_schedule())
+
+        w_units = [(w, j) for j in range(NJ) for w in ("k", "v", "q")]
 
         xs_bc = const.tile([P, D], F32, name="xs_bc")
         nc.scalar.dma_start(out=xs_bc[:], in_=x_scale.rearrange("a b k -> (a b k)").partition_broadcast(P))
@@ -48,7 +52,6 @@ def tile_aftattention_kernel(tc, x_bytes, x_scale, Wq, bq, Wk, bk, Wv, bv, wbias
         xby = []
         w_dram = {"k": Wk, "v": Wv, "q": Wq}
         w_raw = {}
-        w_units = [(w, j) for j in range(NJ) for w in ("k", "v", "q")]
 
         def load_x(q):
             t = keep.tile([P, 2, D], U8, name="x_bytes_sb%d" % q)
@@ -84,7 +87,7 @@ def tile_aftattention_kernel(tc, x_bytes, x_scale, Wq, bq, Wk, bk, Wv, bv, wbias
         nc.gpsimd.tensor_copy(out=brow32[:], in_=brow[:])
 
         def bias_columns():
-            bps = psum.tile([P, P], F32, name="bps", tag="sd", bufs=4)
+            bps = psum.tile([P, P], F32, name="bps", tag="ps", bufs=8)
             nc.tensor.transpose(bps[:], brow32[:], ident[:])
             nc.scalar.copy(out=bcol[:], in_=bps[:, 0 : 4 * NJ])
             nc.gpsimd.tensor_tensor(out=eb[:], in0=bcol[:, 0:NJ], in1=bcol[:, NJ : 2 * NJ], op=ALU.add)
@@ -103,7 +106,7 @@ def tile_aftattention_kernel(tc, x_bytes, x_scale, Wq, bq, Wk, bk, Wv, bv, wbias
         grps = {}
 
         def turn(key, sources):
-            bank = psum.tile([P, 512], F32, name="bank", tag="sd", bufs=4)
+            bank = psum.tile([P, 512], F32, name="bank", tag="ps", bufs=8)
             for n, src in enumerate(sources):
                 nc.tensor.transpose(bank[:, n * P : (n + 1) * P], src, ident[:])
             grp = work.tile([P, 1024], BF16, name="grp", tag="grp", bufs=8, align_bytes=64)
@@ -169,17 +172,17 @@ def tile_aftattention_kernel(tc, x_bytes, x_scale, Wq, bq, Wk, bk, Wv, bv, wbias
         thts = {}
 
         def kproj(j, c):
-            ees[(j, c)] = work.tile([P, 2, CH], F32, name="ee", tag="ee", bufs=4)
-            kps = project("k", j, c, "sd", 4)
+            ees[(j, c)] = work.tile([P, 2, CH], F32, name="ee", tag="ee", bufs=5)
+            kps = project("k", j, c, "ps", 8)
             nc.scalar.activation(out=ees[(j, c)][:, 0, :], in_=kps[:], func=ACT.Exp, bias=eb[:, j : j + 1], scale=1.0)
 
         def vproj(j, c):
-            vpss[(j, c)] = project("v", j, c, "v", 2)
+            vpss[(j, c)] = project("v", j, c, "ps", 8)
 
         def qproj(j, c):
             if c == 0:
                 ths[j] = work.tile([P, B * P], F32, name="th", tag="th", bufs=LAG + 3)
-            qps = project("q", j, c, "sd", 4)
+            qps = project("q", j, c, "ps", 8)
             nc.scalar.activation(
                 out=ths[j][:, c * CH : (c + 1) * CH], in_=qps[:], func=ACT.Tanh, bias=hbq[:, j : j + 1], scale=0.5
             )
@@ -203,26 +206,28 @@ def tile_aftattention_kernel(tc, x_bytes, x_scale, Wq, bq, Wk, bk, Wv, bv, wbias
 
         def t2(j, c, eng):
             a1 = a1s[(j, c)]
-            if c == 0:
-                a2 = work.tile([P, 2, P], F32, name="a2c0", tag="a2c0", bufs=LAG + 3)
-            else:
-                a2 = work.tile([P, 2, P], F32, name="a2c1", tag="a2c1")
+            a2 = work.tile([P, 2, P], F32, name="a2", tag="a2c%d" % c, bufs=LAG + 3)
             eng.tensor_tensor(out=a2[:], in0=a1[:, :, 0:P], in1=a1[:, :, P : 2 * P], op=ALU.add)
             part[(j, c)] = a2
 
         rdens = {}
 
         def back_sums(j):
-            dn = psum.tile([P, 2, P], F32, name="dn", tag="sd", bufs=4)
+            dn = psum.tile([P, 2, P], F32, name="dn", tag="ps", bufs=8)
             for s in range(2):
-                for c in range(NC):
+                blocks = [part[(j, 0)][:, s, :]]
+                if (j, 1) in part:
+                    blocks.append(part[(j, 1)][:, s, :])
+                else:
+                    blocks.extend([ees[(j, 1)][:, s, i * P : (i + 1) * P] for i in range(4)])
+                for i, blk in enumerate(blocks):
                     nc.tensor.matmul(
                         out=dn[:, s, :],
-                        lhsT=part[(j, c)][:, s, :],
+                        lhsT=blk,
                         rhs=ident[:],
                         is_transpose=True,
-                        start=(c == 0),
-                        stop=(c == NC - 1),
+                        start=(i == 0),
+                        stop=(i == len(blocks) - 1),
                     )
             tots[j] = dn
 
@@ -231,19 +236,18 @@ def tile_aftattention_kernel(tc, x_bytes, x_scale, Wq, bq, Wk, bk, Wv, bv, wbias
             nc.vector.reciprocal(out=rdens[j][:], in_=tots[j][:, 0, :])
 
         def whmul(j):
-            wht = work.tile([P, P], F32, name="wht", tag="wht")
+            wht = work.tile([P, P], F32, name="wht", tag="wht", bufs=3)
             nc.vector.scalar_tensor_tensor(
                 out=wht[:], in0=tots[j][:, 1, :], scalar=0.5, in1=rdens[j][:], op0=ALU.mult, op1=ALU.mult
             )
             whts[j] = wht
 
         def back_th(j, c):
-            if True:
-                tht = psum.tile([P, 512], F32, name="tht", tag="tht", bufs=2)
-                for i in range(4):
-                    b = 4 * c + i
-                    nc.tensor.transpose(tht[:, i * P : (i + 1) * P], ths[j][:, b * P : (b + 1) * P], ident[:])
-                thts[(j, c)] = tht
+            tht = psum.tile([P, 512], F32, name="tht", tag="ps", bufs=8)
+            for i in range(4):
+                b = 4 * c + i
+                nc.tensor.transpose(tht[:, i * P : (i + 1) * P], ths[j][:, b * P : (b + 1) * P], ident[:])
+            thts[(j, c)] = tht
 
         outs = {}
 
@@ -251,36 +255,38 @@ def tile_aftattention_kernel(tc, x_bytes, x_scale, Wq, bq, Wk, bk, Wv, bv, wbias
             if c == 0:
                 outs[j] = work.tile([P, B, P], F32, name="o", tag="o", bufs=3)
             o = outs[j]
-            if True:
-                bs = slice(4 * c, 4 * c + 4)
-                nc.vector.scalar_tensor_tensor(
-                    out=o[:, bs, :],
-                    in0=thts[(j, c)][:].rearrange("p (b h) -> p b h", b=4),
-                    scalar=1.0,
-                    in1=whts[j][:].unsqueeze(1).to_broadcast([P, 4, P]),
-                    op0=ALU.add,
-                    op1=ALU.mult,
-                )
-                nc.sync.dma_start(out=out_view[:, bs, j * P : (j + 1) * P], in_=o[:, bs, :])
+            bs = slice(4 * c, 4 * c + 4)
+            nc.vector.scalar_tensor_tensor(
+                out=o[:, bs, :],
+                in0=thts[(j, c)][:].rearrange("p (b h) -> p b h", b=4),
+                scalar=1.0,
+                in1=whts[j][:].unsqueeze(1).to_broadcast([P, 4, P]),
+                op0=ALU.add,
+                op1=ALU.mult,
+            )
+            nc.sync.dma_start(out=out_view[:, bs, j * P : (j + 1) * P], in_=o[:, bs, :])
 
         pos = [0, 0]
 
-        def w_next():
-            if pos[0] < len(w_units):
-                w_turn(*w_units[pos[0]])
-                pos[0] = pos[0] + 1
+        def w_next(k=1):
+            for i in range(k):
+                if pos[0] < len(w_units):
+                    w_turn(*w_units[pos[0]])
+                    pos[0] = pos[0] + 1
 
         def w_quant_turned(limit=99):
             for i in range(pos[1], min(pos[0], pos[1] + limit)):
                 w_quant(*w_units[i])
                 pos[1] = i + 1
 
-        gp = nc.gpsimd
-        ve = nc.vector
+        def sums(j, c):
+            eng = nc.vector if j >= VSUM_FROM else nc.gpsimd
+            t1(j, c, eng)
+            t2(j, c, eng)
+
         widen(0)
         widen(1)
-        w_next()
-        w_next()
+        w_next(2)
         x_turn(0, 0)
         x_turn(0, 1)
         widen(2)
@@ -289,8 +295,7 @@ def tile_aftattention_kernel(tc, x_bytes, x_scale, Wq, bq, Wk, bk, Wv, bv, wbias
         bias_columns()
         x_turn(1, 0)
         x_turn(1, 1)
-        w_next()
-        w_next()
+        w_next(2)
         w_quant_turned(2)
         x_quant(0, 0)
         x_quant(0, 1)
@@ -299,53 +304,61 @@ def tile_aftattention_kernel(tc, x_bytes, x_scale, Wq, bq, Wk, bk, Wv, bv, wbias
         x_quant(1, 1)
         w_quant_turned()
         w_next()
-        V0 = (7,)
-        V1 = (7,)
-        for n in range(NJ + LAG + 1):
+        for n in range(NJ + LAG):
             a = n
             b = n - LAG
             r = b - 1
+            early = b == NJ - 2
+            final = b == NJ - 1
             if a < NJ:
                 kproj(a, 0)
-                vproj(a, 0)
                 qproj(a, 0)
-            if 0 <= b < NJ:
+                vproj(a, 0)
+            if 0 <= b < NJ and not final:
                 kproj(b, 1)
+                qproj(b, 1)
                 vproj(b, 1)
+            if early:
+                kproj(b + 1, 1)
+                vproj(b + 1, 1)
+            if final:
                 qproj(b, 1)
             if n < 2:
                 widen(4 + 2 * n)
                 widen(5 + 2 * n)
-            if n == 0:
-                w_quant_turned()
+            w_quant_turned()
             if a < NJ:
                 ev(a, 0)
-                e0 = ve if a in V0 else gp
-                t1(a, 0, e0)
-                t2(a, 0, e0)
-            if 0 <= b < NJ:
+                sums(a, 0)
+            if 0 <= b < NJ and not final:
                 ev(b, 1)
-            if 0 <= b < NJ:
-                e1 = ve if b in V1 else gp
-                t1(b, 1, e1)
-                t2(b, 1, e1)
+                if b < TSUM_FROM:
+                    sums(b, 1)
+            if early:
+                ev(b + 1, 1)
             if 0 <= r < NJ:
                 back_sums(r)
-            w_next()
-            w_next()
-            w_next()
+                recip(r)
+                whmul(r)
+            w_next(3)
             if n < 2:
                 x_turn(2 + n, 0)
                 x_turn(2 + n, 1)
             if 0 <= r < NJ:
                 back_th(r, 0)
                 back_th(r, 1)
-                recip(r)
-                whmul(r)
-            w_quant_turned()
             if n < 2:
+                w_quant_turned()
                 x_quant(2 + n, 0)
                 x_quant(2 + n, 1)
             if 0 <= r < NJ:
                 fin(r, 0)
                 fin(r, 1)
+            if final:
+                back_sums(b)
+                recip(b)
+                whmul(b)
+                back_th(b, 0)
+                back_th(b, 1)
+                fin(b, 0)
+                fin(b, 1)

@@ -27,6 +27,7 @@ LAG = 2
 WFIRST = 4
 TSUM_FROM = 6
 VSUM_FROM = 7
+SORT_FROM = 4
 
 
 def tile_aftattention_kernel(tc, x_bytes, x_scale, Wq, bq, Wk, bk, Wv, bv, wbias, out):
@@ -105,30 +106,47 @@ def tile_aftattention_kernel(tc, x_bytes, x_scale, Wq, bq, Wk, bk, Wv, bv, wbias
         wsc = {}
         grps = {}
 
-        def turn(key, sources):
+        def turn(dest, sources):
             bank = psum.tile([P, 512], F32, name="bank", tag="ps", bufs=8)
             for n, src in enumerate(sources):
                 nc.tensor.transpose(bank[:, n * P : (n + 1) * P], src, ident[:])
-            grp = work.tile([P, 1024], BF16, name="grp", tag="grp", bufs=8, align_bytes=64)
             nc.scalar.copy(
-                out=grp[:].bitcast(F32).rearrange("p (i r u) -> p i r u", i=2, u=2),
+                out=dest.bitcast(F32).rearrange("p (i r u) -> p i r u", i=2, u=2),
                 in_=bank[:].rearrange("p (i u r) -> p i r u", i=2, u=2),
             )
-            grps[key] = grp
 
         def every_second(words, g, u):
             return words[:, 256 * g + u : 256 * (g + 1) : 2]
 
-        def w_turn(w, j):
-            words = w_raw[(w, j)][:].bitcast(F32)
-            turn((w, j), [every_second(words, g, u) for g in range(NG) for u in range(2)])
+        w_sorted = {}
 
-        def w_quant(w, j):
-            c_t = keep.tile([P, 256], U32, name="wc_%s%d" % (w, j), align_bytes=64)
-            s_t = keep.tile([P, 256], U8, name="wsc_%s%d" % (w, j), align_bytes=64)
-            wc[(w, j)] = c_t
-            wsc[(w, j)] = s_t
-            nc.vector.quantize_mx(out=c_t[:].bitcast(FP8X4), scales=s_t[:], in_=grps[(w, j)][:])
+        def w_sort(w, j):
+            t = work.tile([P, D // 2], F32, name="wsort", tag="wsort", bufs=6)
+            nc.vector.tensor_copy(
+                out=t[:].rearrange("p (g u r) -> p g u r", g=NG, u=2),
+                in_=w_raw[(w, j)][:].bitcast(F32).rearrange("p (g r u) -> p g u r", g=NG, u=2),
+            )
+            w_sorted[(w, j)] = t
+
+        def w_turn(w, j):
+            if w == "k":
+                grps[("kv", j)] = work.tile([P, 2048], BF16, name="grp2", tag="grp2", bufs=4, align_bytes=64)
+            if w == "q":
+                grps[("q", j)] = work.tile([P, 1024], BF16, name="grp1", tag="grp1", bufs=4, align_bytes=64)
+            dest = grps[("q", j)][:] if w == "q" else grps[("kv", j)][:, 1024 * "kv".index(w) : 1024 * "kv".index(w) + 1024]
+            if (w, j) in w_sorted:
+                turn(dest, [w_sorted[(w, j)][:, n * P : (n + 1) * P] for n in range(2 * NG)])
+            else:
+                words = w_raw[(w, j)][:].bitcast(F32)
+                turn(dest, [every_second(words, g, u) for g in range(NG) for u in range(2)])
+
+        def w_quant(ws, j):
+            c_t = keep.tile([P, 256 * len(ws)], U32, name="wc_%s%d" % (ws, j), align_bytes=64)
+            s_t = keep.tile([P, 256 * len(ws)], U8, name="wsc_%s%d" % (ws, j), align_bytes=64)
+            for i, w in enumerate(ws):
+                wc[(w, j)] = c_t[:, 256 * i : 256 * i + 256]
+                wsc[(w, j)] = s_t[:, 256 * i : 256 * i + 256]
+            nc.vector.quantize_mx(out=c_t[:].bitcast(FP8X4), scales=s_t[:], in_=grps[(ws, j)][:])
 
         xb = {}
 
@@ -138,14 +156,14 @@ def tile_aftattention_kernel(tc, x_bytes, x_scale, Wq, bq, Wk, bk, Wv, bv, wbias
             xb[b] = t
 
         def x_turn(q, g):
-            turn(("x", q, g), [every_second(xb[2 * q + i][:].bitcast(F32), g, u) for i in range(2) for u in range(2)])
-
-        def x_quant(q, g):
             c = q // 2
-            cols = slice((q % 2) * 256, (q % 2) * 256 + 256)
-            nc.vector.quantize_mx(
-                out=xc[(g, c)][:, cols].bitcast(FP8X4), scales=xsc[(g, c)][:, cols], in_=grps[("x", q, g)][:]
-            )
+            if q % 2 == 0:
+                grps[("x", g, c)] = work.tile([P, 2048], BF16, name="grpx", tag="grpx", bufs=4, align_bytes=64)
+            dest = grps[("x", g, c)][:, 1024 * (q % 2) : 1024 * (q % 2) + 1024]
+            turn(dest, [every_second(xb[2 * q + i][:].bitcast(F32), g, u) for i in range(2) for u in range(2)])
+
+        def x_quant(g, c):
+            nc.vector.quantize_mx(out=xc[(g, c)][:].bitcast(FP8X4), scales=xsc[(g, c)][:], in_=grps[("x", g, c)][:])
 
         def project(w, j, c, tag, bufs):
             acc = psum.tile([P, CH], F32, name="acc", tag=tag, bufs=bufs)
@@ -274,10 +292,14 @@ def tile_aftattention_kernel(tc, x_bytes, x_scale, Wq, bq, Wk, bk, Wv, bv, wbias
                     w_turn(*w_units[pos[0]])
                     pos[0] = pos[0] + 1
 
+        q_units = [(ws, j) for j in range(NJ) for ws in ("kv", "q")]
+
         def w_quant_turned(limit=99):
-            for i in range(pos[1], min(pos[0], pos[1] + limit)):
-                w_quant(*w_units[i])
-                pos[1] = i + 1
+            for i in range(pos[1], min(len(q_units), pos[1] + limit)):
+                ws, j = q_units[i]
+                if pos[0] > 3 * j + (1 if ws == "kv" else 2):
+                    w_quant(ws, j)
+                    pos[1] = i + 1
 
         def sums(j, c):
             eng = nc.vector if j >= VSUM_FROM else nc.gpsimd
@@ -298,10 +320,7 @@ def tile_aftattention_kernel(tc, x_bytes, x_scale, Wq, bq, Wk, bk, Wv, bv, wbias
         w_next(2)
         w_quant_turned(2)
         x_quant(0, 0)
-        x_quant(0, 1)
-        w_quant_turned(1)
         x_quant(1, 0)
-        x_quant(1, 1)
         w_quant_turned()
         w_next()
         for n in range(NJ + LAG):
@@ -330,6 +349,9 @@ def tile_aftattention_kernel(tc, x_bytes, x_scale, Wq, bq, Wk, bk, Wv, bv, wbias
             if a < NJ:
                 ev(a, 0)
                 sums(a, 0)
+            for unit in w_units[pos[0] : pos[0] + 3]:
+                if unit[1] >= SORT_FROM:
+                    w_sort(*unit)
             if 0 <= b < NJ and not final:
                 ev(b, 1)
                 if b < TSUM_FROM:
@@ -349,8 +371,9 @@ def tile_aftattention_kernel(tc, x_bytes, x_scale, Wq, bq, Wk, bk, Wv, bv, wbias
                 back_th(r, 1)
             if n < 2:
                 w_quant_turned()
-                x_quant(2 + n, 0)
-                x_quant(2 + n, 1)
+            if n == 1:
+                x_quant(0, 1)
+                x_quant(1, 1)
             if 0 <= r < NJ:
                 fin(r, 0)
                 fin(r, 1)

@@ -26,7 +26,8 @@ NG = 2
 LAG = 2
 WFIRST = 4
 TSUM_FROM = 6
-VSUM_FROM = 7
+VSUM_FROM = 8
+FIN_ELSEWHERE = ((5, 0), (5, 1), (6, 0))
 SORT_FROM = 4
 
 
@@ -121,7 +122,7 @@ def tile_aftattention_kernel(tc, x_bytes, x_scale, Wq, bq, Wk, bk, Wv, bv, wbias
         w_sorted = {}
 
         def w_sort(w, j):
-            t = work.tile([P, D // 2], F32, name="wsort", tag="wsort", bufs=6)
+            t = work.tile([P, D // 2], F32, name="wsort", tag="wsort", bufs=4)
             nc.vector.tensor_copy(
                 out=t[:].rearrange("p (g u r) -> p g u r", g=NG, u=2),
                 in_=w_raw[(w, j)][:].bitcast(F32).rearrange("p (g r u) -> p g u r", g=NG, u=2),
@@ -274,14 +275,23 @@ def tile_aftattention_kernel(tc, x_bytes, x_scale, Wq, bq, Wk, bk, Wv, bv, wbias
                 outs[j] = work.tile([P, B, P], F32, name="o", tag="o", bufs=3)
             o = outs[j]
             bs = slice(4 * c, 4 * c + 4)
-            nc.vector.scalar_tensor_tensor(
-                out=o[:, bs, :],
-                in0=thts[(j, c)][:].rearrange("p (b h) -> p b h", b=4),
-                scalar=1.0,
-                in1=whts[j][:].unsqueeze(1).to_broadcast([P, 4, P]),
-                op0=ALU.add,
-                op1=ALU.mult,
-            )
+            if (j, c) in FIN_ELSEWHERE:
+                th1 = work.tile([P, 4, P], F32, name="th1", tag="th1", bufs=2)
+                nc.scalar.activation(
+                    out=th1[:], in_=thts[(j, c)][:].rearrange("p (b h) -> p b h", b=4), func=ACT.Copy, bias=1.0, scale=1.0
+                )
+                nc.gpsimd.tensor_tensor(
+                    out=o[:, bs, :], in0=th1[:], in1=whts[j][:].unsqueeze(1).to_broadcast([P, 4, P]), op=ALU.mult
+                )
+            else:
+                nc.vector.scalar_tensor_tensor(
+                    out=o[:, bs, :],
+                    in0=thts[(j, c)][:].rearrange("p (b h) -> p b h", b=4),
+                    scalar=1.0,
+                    in1=whts[j][:].unsqueeze(1).to_broadcast([P, 4, P]),
+                    op0=ALU.add,
+                    op1=ALU.mult,
+                )
             nc.sync.dma_start(out=out_view[:, bs, j * P : (j + 1) * P], in_=o[:, bs, :])
 
         pos = [0, 0]

@@ -220,14 +220,15 @@ def tile_aftattention_kernel(tc, x_bytes, x_scale, Wq, bq, Wk, bk, Wv, bv, wbias
 
         def t1(j, c, eng):
             ee = ees[(j, c)]
-            a1s[(j, c)] = work.tile([P, 2, 256], F32, name="a1", tag="a1", bufs=3)
+            a1s[(j, c)] = work.tile([P, 2, 256], F32, name="a1", tag="a1", bufs=4)
             eng.tensor_tensor(out=a1s[(j, c)][:], in0=ee[:, :, 0:256], in1=ee[:, :, 256:512], op=ALU.add)
+            part[(j, c)] = a1s[(j, c)][:]
 
         def t2(j, c, eng):
             a1 = a1s[(j, c)]
             a2 = work.tile([P, 2, P], F32, name="a2", tag="a2c%d" % c, bufs=LAG + 3)
             eng.tensor_tensor(out=a2[:], in0=a1[:, :, 0:P], in1=a1[:, :, P : 2 * P], op=ALU.add)
-            part[(j, c)] = a2
+            part[(j, c)] = a2[:]
 
         rdens = {}
 
@@ -236,7 +237,7 @@ def tile_aftattention_kernel(tc, x_bytes, x_scale, Wq, bq, Wk, bk, Wv, bv, wbias
             for s in range(2):
                 blocks = [part[(j, 0)][:, s, :]]
                 if (j, 1) in part:
-                    blocks.append(part[(j, 1)][:, s, :])
+                    blocks.extend([part[(j, 1)][:, s, i * P : (i + 1) * P] for i in range(2)])
                 else:
                     blocks.extend([ees[(j, 1)][:, s, i * P : (i + 1) * P] for i in range(4)])
                 for i, blk in enumerate(blocks):
@@ -314,7 +315,8 @@ def tile_aftattention_kernel(tc, x_bytes, x_scale, Wq, bq, Wk, bk, Wv, bv, wbias
         def sums(j, c):
             eng = nc.vector if j >= VSUM_FROM else nc.gpsimd
             t1(j, c, eng)
-            t2(j, c, eng)
+            if c == 0:
+                t2(j, c, eng)
 
         widen(0)
         widen(1)

@@ -220,7 +220,7 @@ def tile_aftattention_kernel(tc, x_bytes, x_scale, Wq, bq, Wk, bk, Wv, bv, wbias
 
         def t1(j, c, eng):
             ee = ees[(j, c)]
-            a1s[(j, c)] = work.tile([P, 2, 256], F32, name="a1", tag="a1", bufs=4)
+            a1s[(j, c)] = work.tile([P, 2, 256], F32, name="a1", tag="a1c%d" % c, bufs=LAG + 3 if c == 0 else 3)
             eng.tensor_tensor(out=a1s[(j, c)][:], in0=ee[:, :, 0:256], in1=ee[:, :, 256:512], op=ALU.add)
             part[(j, c)] = a1s[(j, c)][:]
 
@@ -235,9 +235,9 @@ def tile_aftattention_kernel(tc, x_bytes, x_scale, Wq, bq, Wk, bk, Wv, bv, wbias
         def back_sums(j):
             dn = psum.tile([P, 2, P], F32, name="dn", tag="ps", bufs=8)
             for s in range(2):
-                blocks = [part[(j, 0)][:, s, :]]
+                blocks = [part[(j, 0)][:, s, i * P : (i + 1) * P] for i in range(2)]
                 if (j, 1) in part:
-                    blocks.extend([part[(j, 1)][:, s, i * P : (i + 1) * P] for i in range(2)])
+                    blocks.append(part[(j, 1)][:, s, :])
                 else:
                     blocks.extend([ees[(j, 1)][:, s, i * P : (i + 1) * P] for i in range(4)])
                 for i, blk in enumerate(blocks):
@@ -315,7 +315,7 @@ def tile_aftattention_kernel(tc, x_bytes, x_scale, Wq, bq, Wk, bk, Wv, bv, wbias
         def sums(j, c):
             eng = nc.vector if j >= VSUM_FROM else nc.gpsimd
             t1(j, c, eng)
-            if c == 0:
+            if c == 1:
                 t2(j, c, eng)
 
         widen(0)

@@ -22,6 +22,7 @@ NJ = H // P
 CH = 512
 NC = 2
 NG = 2
+NS = 8
 
 LAG = 2
 WFIRST = 4
@@ -42,13 +43,19 @@ def tile_aftattention_kernel(tc, x_bytes, x_scale, Wq, bq, Wk, bk, Wv, bv, wbias
 
         w_units = [(w, j) for j in range(NJ) for w in ("k", "v", "q")]
 
-        xs_bc = const.tile([P, D], F32, name="xs_bc")
-        nc.scalar.dma_start(out=xs_bc[:], in_=x_scale.rearrange("a b k -> (a b k)").partition_broadcast(P))
+        warm = const.tile([P, 1], F32, name="warm")
+        nc.gpsimd.memset(warm[:], 0.0)
+        warm2 = const.tile([P, 1], F32, name="warm2")
+        nc.scalar.activation(out=warm2[:], in_=warm[:], func=ACT.Exp)
+
+        scol = const.tile([P, NS], F32, name="scol")
+        nc.sync.dma_start(out=scol[:], in_=x_scale.rearrange("a b (p j) -> (a b p) j", j=NS))
 
         brow = const.tile([P, P], BF16, name="brow")
         nc.gpsimd.memset(brow[:], 0.0)
-        for v, vec in enumerate((bk, wbias, bv, bq)):
-            nc.scalar.dma_start(out=brow[NJ * v : NJ * (v + 1), :], in_=vec.rearrange("(c p) -> c p", p=P))
+
+        ident = const.tile([P, P], F32, name="ident")
+        make_identity(nc, ident[:])
 
         x_view = x_bytes.rearrange("b t k -> t b k")
         xby = []
@@ -69,26 +76,22 @@ def tile_aftattention_kernel(tc, x_bytes, x_scale, Wq, bq, Wk, bk, Wv, bv, wbias
         load_x(1)
         for unit in w_units[:WFIRST]:
             load_w(*unit)
+        for v, vec in enumerate((bk, wbias, bv, bq)):
+            nc.sync.dma_start(out=brow[NJ * v : NJ * (v + 1), :], in_=vec.rearrange("(c p) -> c p", p=P))
         load_x(2)
         load_x(3)
         for unit in w_units[WFIRST:]:
             load_w(*unit)
 
-        warm = const.tile([P, 1], F32, name="warm")
-        nc.gpsimd.memset(warm[:], 0.0)
-        ident = const.tile([P, P], F32, name="ident")
-        make_identity(nc, ident[:])
-        warm2 = const.tile([P, 1], F32, name="warm2")
-        nc.scalar.activation(out=warm2[:], in_=warm[:], func=ACT.Exp)
 
         bcol = const.tile([P, 4 * NJ], F32, name="bcol")
         eb = const.tile([P, NJ], F32, name="eb")
         bvf = bcol[:, 2 * NJ : 3 * NJ]
         hbq = const.tile([P, NJ], F32, name="hbq")
         brow32 = const.tile([P, P], F32, name="brow32")
-        nc.gpsimd.tensor_copy(out=brow32[:], in_=brow[:])
 
         def bias_columns():
+            nc.scalar.copy(out=brow32[:], in_=brow[:])
             bps = psum.tile([P, P], F32, name="bps", tag="ps", bufs=8)
             nc.tensor.transpose(bps[:], brow32[:], ident[:])
             nc.scalar.copy(out=bcol[:], in_=bps[:, 0 : 4 * NJ])
@@ -96,6 +99,16 @@ def tile_aftattention_kernel(tc, x_bytes, x_scale, Wq, bq, Wk, bk, Wv, bv, wbias
             nc.gpsimd.tensor_scalar(
                 out=hbq[:], in0=bcol[:, 3 * NJ : 4 * NJ], scalar1=0.5, scalar2=0.0, op0=ALU.mult, op1=ALU.add
             )
+
+        xs_bc = const.tile([P, D], F32, name="xs_bc")
+        xs_view = xs_bc[:].rearrange("p (n j) -> p n j", j=NS)
+        for h in range(2):
+            sbank = psum.tile([P, 512], F32, name="sbank", tag="ps", bufs=8)
+            for n in range(4):
+                j = 4 * h + n
+                nc.tensor.transpose(sbank[:, n * P : (n + 1) * P], scol[:, j : j + 1].to_broadcast([P, P]), ident[:])
+            copy = nc.scalar.copy if h == 0 else nc.vector.tensor_copy
+            copy(out=xs_view[:, :, 4 * h : 4 * h + 4], in_=sbank[:].rearrange("p (j n) -> p n j", j=4))
 
         xc = {}
         xsc = {}

@@ -56,6 +56,8 @@ def tile_aftattention_kernel(tc, x_bytes, x_scale, Wq, bq, Wk, bk, Wv, bv, wbias
 
         ident = const.tile([P, P], F32, name="ident")
         make_identity(nc, ident[:])
+        ident16 = const.tile([P, P], BF16, name="ident16")
+        make_identity(nc, ident16[:])
 
         x_view = x_bytes.rearrange("b t k -> t b k")
         xby = []
@@ -88,12 +90,10 @@ def tile_aftattention_kernel(tc, x_bytes, x_scale, Wq, bq, Wk, bk, Wv, bv, wbias
         eb = const.tile([P, NJ], F32, name="eb")
         bvf = bcol[:, 2 * NJ : 3 * NJ]
         hbq = const.tile([P, NJ], F32, name="hbq")
-        brow32 = const.tile([P, P], F32, name="brow32")
 
         def bias_columns():
-            nc.scalar.copy(out=brow32[:], in_=brow[:])
-            bps = psum.tile([P, P], F32, name="bps", tag="ps", bufs=8)
-            nc.tensor.transpose(bps[:], brow32[:], ident[:])
+            bps = psum.tile([P, P], BF16, name="bps", tag="ps", bufs=8)
+            nc.tensor.transpose(bps[:], brow[:], ident16[:])
             nc.scalar.copy(out=bcol[:], in_=bps[:, 0 : 4 * NJ])
             nc.gpsimd.tensor_tensor(out=eb[:], in0=bcol[:, 0:NJ], in1=bcol[:, NJ : 2 * NJ], op=ALU.add)
             nc.gpsimd.tensor_scalar(
@@ -339,9 +339,9 @@ def tile_aftattention_kernel(tc, x_bytes, x_scale, Wq, bq, Wk, bk, Wv, bv, wbias
         widen(2)
         widen(3)
         w_next()
-        bias_columns()
         x_turn(1, 0)
         x_turn(1, 1)
+        bias_columns()
         w_next(2)
         w_quant_turned(2)
         x_quant(0, 0)
@@ -358,6 +358,8 @@ def tile_aftattention_kernel(tc, x_bytes, x_scale, Wq, bq, Wk, bk, Wv, bv, wbias
                 kproj(a, 0)
                 qproj(a, 0)
                 vproj(a, 0)
+            w_quant_turned()
+            w_next(3)
             if 0 <= b < NJ and not final:
                 kproj(b, 1)
                 qproj(b, 1)
@@ -370,7 +372,6 @@ def tile_aftattention_kernel(tc, x_bytes, x_scale, Wq, bq, Wk, bk, Wv, bv, wbias
             if n < 2:
                 widen(4 + 2 * n)
                 widen(5 + 2 * n)
-            w_quant_turned()
             if a < NJ:
                 ev(a, 0)
                 sums(a, 0)
@@ -387,7 +388,6 @@ def tile_aftattention_kernel(tc, x_bytes, x_scale, Wq, bq, Wk, bk, Wv, bv, wbias
                 back_sums(r)
                 recip(r)
                 whmul(r)
-            w_next(3)
             if n < 2:
                 x_turn(2 + n, 0)
                 x_turn(2 + n, 1)

from contextlib import ExitStack

import concourse.mybir as mybir
from concourse.masks import make_identity

FLOPS = 2 * 3 * 1024 * 1024 * 1024

F32 = mybir.dt.float32
BF16 = mybir.dt.bfloat16
U32 = mybir.dt.uint32
U8 = mybir.dt.uint8
FP8 = mybir.dt.float8_e4m3fn
FP8X4 = mybir.dt.float8_e4m3fn_x4
ALU = mybir.AluOpType
ACT = mybir.ActivationFunctionType

P = 128
B = 8
D = 1024
H = 1024
NJ = H // P
CH = 512
NC = 2
NG = 2
NS = 8

LAG = 2
WFIRST = 4
TSUM_FROM = 6
VSUM_FROM = 8
FIN_ELSEWHERE = ((5, 0), (5, 1), (6, 0))
SORT_FROM = 4


def tile_aftattention_kernel(tc, x_bytes, x_scale, Wq, bq, Wk, bk, Wv, bv, wbias, out):
    nc = tc.nc
    with ExitStack() as ctx:
        const = ctx.enter_context(tc.tile_pool(name="const", bufs=1))
        keep = ctx.enter_context(tc.tile_pool(name="keep", bufs=1))
        work = ctx.enter_context(tc.tile_pool(name="work", bufs=2))
        psum = ctx.enter_context(tc.psum_pool(name="psum", bufs=2))
        ctx.enter_context(tc.manual_schedule())

        w_units = [(w, j) for j in range(NJ) for w in ("k", "v", "q")]

        warm = const.tile([P, 1], F32, name="warm")
        nc.gpsimd.memset(warm[:], 0.0)
        warm2 = const.tile([P, 1], F32, name="warm2")
        nc.scalar.activation(out=warm2[:], in_=warm[:], func=ACT.Exp)

        scol = const.tile([P, NS], F32, name="scol")
        nc.sync.dma_start(out=scol[:], in_=x_scale.rearrange("a b (p j) -> (a b p) j", j=NS))

        brow = const.tile([P, P], BF16, name="brow")
        nc.gpsimd.memset(brow[:], 0.0)

        ident = const.tile([P, P], F32, name="ident")
        make_identity(nc, ident[:])
        ident16 = const.tile([P, P], BF16, name="ident16")
        make_identity(nc, ident16[:])

        x_view = x_bytes.rearrange("b t k -> t b k")
        xby = []
        w_dram = {"k": Wk, "v": Wv, "q": Wq}
        w_raw = {}

        def load_x(q):
            t = keep.tile([P, 2, D], U8, name="x_bytes_sb%d" % q)
            nc.sync.dma_start(out=t[:], in_=x_view[:, 2 * q : 2 * q + 2, :])
            xby.append(t)

        def load_w(w, j):
            t = keep.tile([P, D], BF16, name="wraw_%s%d" % (w, j))
            nc.sync.dma_start(out=t[:], in_=w_dram[w][j * P : (j + 1) * P, :])
            w_raw[(w, j)] = t

        load_x(0)
        load_x(1)
        for unit in w_units[:WFIRST]:
            load_w(*unit)
        for v, vec in enumerate((bk, wbias, bv, bq)):
            nc.sync.dma_start(out=brow[NJ * v : NJ * (v + 1), :], in_=vec.rearrange("(c p) -> c p", p=P))
        load_x(2)
        load_x(3)
        for unit in w_units[WFIRST:]:
            load_w(*unit)


        bcol = const.tile([P, 4 * NJ], F32, name="bcol")
        eb = const.tile([P, NJ], F32, name="eb")
        bvf = bcol[:, 2 * NJ : 3 * NJ]
        hbq = const.tile([P, NJ], F32, name="hbq")

        def bias_columns():
            bps = psum.tile([P, P], BF16, name="bps", tag="ps", bufs=8)
            nc.tensor.transpose(bps[:], brow[:], ident16[:])
            nc.scalar.copy(out=bcol[:], in_=bps[:, 0 : 4 * NJ])
            nc.gpsimd.tensor_tensor(out=eb[:], in0=bcol[:, 0:NJ], in1=bcol[:, NJ : 2 * NJ], op=ALU.add)
            nc.gpsimd.tensor_scalar(
                out=hbq[:], in0=bcol[:, 3 * NJ : 4 * NJ], scalar1=0.5, scalar2=0.0, op0=ALU.mult, op1=ALU.add
            )

        xs_bc = const.tile([P, D], F32, name="xs_bc")
        xs_view = xs_bc[:].rearrange("p (n j) -> p n j", j=NS)
        for h in range(2):
            sbank = psum.tile([P, 512], F32, name="sbank", tag="ps", bufs=8)
            for n in range(4):
                j = 4 * h + n
                nc.tensor.transpose(sbank[:, n * P : (n + 1) * P], scol[:, j : j + 1].to_broadcast([P, P]), ident[:])
            copy = nc.scalar.copy if h == 0 else nc.vector.tensor_copy
            copy(out=xs_view[:, :, 4 * h : 4 * h + 4], in_=sbank[:].rearrange("p (j n) -> p n j", j=4))

        xc = {}
        xsc = {}
        for g in range(NG):
            for c in range(NC):
                xc[(g, c)] = keep.tile([P, CH], U32, name="xc_%d_%d" % (g, c), align_bytes=64)
                xsc[(g, c)] = keep.tile([P, CH], U8, name="xsc_%d_%d" % (g, c), align_bytes=64)
        wc = {}
        wsc = {}
        grps = {}

        def turn(dest, sources):
            bank = psum.tile([P, 512], F32, name="bank", tag="ps", bufs=8)
            for n, src in enumerate(sources):
                nc.tensor.transpose(bank[:, n * P : (n + 1) * P], src, ident[:])
            nc.scalar.copy(
                out=dest.bitcast(F32).rearrange("p (i r u) -> p i r u", i=2, u=2),
                in_=bank[:].rearrange("p (i u r) -> p i r u", i=2, u=2),
            )

        def every_second(words, g, u):
            return words[:, 256 * g + u : 256 * (g + 1) : 2]

        w_sorted = {}

        def w_sort(w, j):
            t = work.tile([P, D // 2], F32, name="wsort", tag="wsort", bufs=4)
            nc.vector.tensor_copy(
                out=t[:].rearrange("p (g u r) -> p g u r", g=NG, u=2),
                in_=w_raw[(w, j)][:].bitcast(F32).rearrange("p (g r u) -> p g u r", g=NG, u=2),
            )
            w_sorted[(w, j)] = t

        def w_turn(w, j):
            if w == "k":
                grps[("kv", j)] = work.tile([P, 2048], BF16, name="grp2", tag="grp2", bufs=4, align_bytes=64)
            if w == "q":
                grps[("q", j)] = work.tile([P, 1024], BF16, name="grp1", tag="grp1", bufs=4, align_bytes=64)
            dest = grps[("q", j)][:] if w == "q" else grps[("kv", j)][:, 1024 * "kv".index(w) : 1024 * "kv".index(w) + 1024]
            if (w, j) in w_sorted:
                turn(dest, [w_sorted[(w, j)][:, n * P : (n + 1) * P] for n in range(2 * NG)])
            else:
                words = w_raw[(w, j)][:].bitcast(F32)
                turn(dest, [every_second(words, g, u) for g in range(NG) for u in range(2)])

        def w_quant(ws, j):
            c_t = keep.tile([P, 256 * len(ws)], U32, name="wc_%s%d" % (ws, j), align_bytes=64)
            s_t = keep.tile([P, 256 * len(ws)], U8, name="wsc_%s%d" % (ws, j), align_bytes=64)
            for i, w in enumerate(ws):
                wc[(w, j)] = c_t[:, 256 * i : 256 * i + 256]
                wsc[(w, j)] = s_t[:, 256 * i : 256 * i + 256]
            nc.vector.quantize_mx(out=c_t[:].bitcast(FP8X4), scales=s_t[:], in_=grps[(ws, j)][:])

        xb = {}

        def widen(b):
            t = work.tile([P, D], BF16, name="xb", tag="xb", bufs=4)
            nc.vector.tensor_tensor(out=t[:], in0=xby[b // 2][:, b % 2, :].bitcast(FP8), in1=xs_bc[:], op=ALU.mult)
            xb[b] = t

        def x_turn(q, g):
            c = q // 2
            if q % 2 == 0:
                grps[("x", g, c)] = work.tile([P, 2048], BF16, name="grpx", tag="grpx", bufs=4, align_bytes=64)
            dest = grps[("x", g, c)][:, 1024 * (q % 2) : 1024 * (q % 2) + 1024]
            turn(dest, [every_second(xb[2 * q + i][:].bitcast(F32), g, u) for i in range(2) for u in range(2)])

        def x_quant(g, c):
            nc.vector.quantize_mx(out=xc[(g, c)][:].bitcast(FP8X4), scales=xsc[(g, c)][:], in_=grps[("x", g, c)][:])

        def project(w, j, c, tag, bufs):
            acc = psum.tile([P, CH], F32, name="acc", tag=tag, bufs=bufs)
            for g in range(NG):
                gs = slice(g * P, (g + 1) * P)
                nc.tensor.matmul_mx(
                    out=acc[:],
                    lhsT=wc[(w, j)][:, gs].bitcast(FP8X4),
                    lhsT_scale=wsc[(w, j)][:, gs],
                    rhs=xc[(g, c)][:].bitcast(FP8X4),
                    rhs_scale=xsc[(g, c)][:],
                    start=(g == 0),
                    stop=(g == NG - 1),
                )
            return acc

        out_view = out.rearrange("b t h -> t b h")
        ees = {}
        ths = {}
        vpss = {}
        part = {}
        tots = {}
        whts = {}
        thts = {}

        def kproj(j, c):
            ees[(j, c)] = work.tile([P, 2, CH], F32, name="ee", tag="ee", bufs=5)
            kps = project("k", j, c, "ps", 8)
            nc.scalar.activation(out=ees[(j, c)][:, 0, :], in_=kps[:], func=ACT.Exp, bias=eb[:, j : j + 1], scale=1.0)

        def vproj(j, c):
            vpss[(j, c)] = project("v", j, c, "ps", 8)

        def qproj(j, c):
            if c == 0:
                ths[j] = work.tile([P, B * P], F32, name="th", tag="th", bufs=LAG + 3)
            qps = project("q", j, c, "ps", 8)
            nc.scalar.activation(
                out=ths[j][:, c * CH : (c + 1) * CH], in_=qps[:], func=ACT.Tanh, bias=hbq[:, j : j + 1], scale=0.5
            )

        def ev(j, c):
            nc.vector.scalar_tensor_tensor(
                out=ees[(j, c)][:, 1, :],
                in0=vpss[(j, c)][:],
                scalar=bvf[:, j : j + 1],
                in1=ees[(j, c)][:, 0, :],
                op0=ALU.add,
                op1=ALU.mult,
            )

        a1s = {}

        def t1(j, c, eng):
            ee = ees[(j, c)]
            a1s[(j, c)] = work.tile([P, 2, 256], F32, name="a1", tag="a1c%d" % c, bufs=LAG + 3 if c == 0 else 3)
            eng.tensor_tensor(out=a1s[(j, c)][:], in0=ee[:, :, 0:256], in1=ee[:, :, 256:512], op=ALU.add)
            part[(j, c)] = a1s[(j, c)][:]

        def t2(j, c, eng):
            a1 = a1s[(j, c)]
            a2 = work.tile([P, 2, P], F32, name="a2", tag="a2c%d" % c, bufs=LAG + 3)
            eng.tensor_tensor(out=a2[:], in0=a1[:, :, 0:P], in1=a1[:, :, P : 2 * P], op=ALU.add)
            part[(j, c)] = a2[:]

        rdens = {}

        def back_sums(j):
            dn = psum.tile([P, 2, P], F32, name="dn", tag="ps", bufs=8)
            for s in range(2):
                blocks = [part[(j, 0)][:, s, i * P : (i + 1) * P] for i in range(2)]
                if (j, 1) in part:
                    blocks.append(part[(j, 1)][:, s, :])
                else:
                    blocks.extend([ees[(j, 1)][:, s, i * P : (i + 1) * P] for i in range(4)])
                for i, blk in enumerate(blocks):
                    nc.tensor.matmul(
                        out=dn[:, s, :],
                        lhsT=blk,
                        rhs=ident[:],
                        is_transpose=True,
                        start=(i == 0),
                        stop=(i == len(blocks) - 1),
                    )
            tots[j] = dn

        def recip(j):
            rdens[j] = work.tile([P, P], F32, name="rden", tag="rden")
            nc.vector.reciprocal(out=rdens[j][:], in_=tots[j][:, 0, :])

        def whmul(j):
            wht = work.tile([P, P], F32, name="wht", tag="wht", bufs=3)
            nc.vector.scalar_tensor_tensor(
                out=wht[:], in0=tots[j][:, 1, :], scalar=0.5, in1=rdens[j][:], op0=ALU.mult, op1=ALU.mult
            )
            whts[j] = wht

        def back_th(j, c):
            tht = psum.tile([P, 512], F32, name="tht", tag="ps", bufs=8)
            for i in range(4):
                b = 4 * c + i
                nc.tensor.transpose(tht[:, i * P : (i + 1) * P], ths[j][:, b * P : (b + 1) * P], ident[:])
            thts[(j, c)] = tht

        outs = {}

        def fin(j, c):
            if c == 0:
                outs[j] = work.tile([P, B, P], F32, name="o", tag="o", bufs=3)
            o = outs[j]
            bs = slice(4 * c, 4 * c + 4)
            if (j, c) in FIN_ELSEWHERE:
                th1 = work.tile([P, 4, P], F32, name="th1", tag="th1", bufs=2)
                nc.scalar.activation(
                    out=th1[:], in_=thts[(j, c)][:].rearrange("p (b h) -> p b h", b=4), func=ACT.Copy, bias=1.0, scale=1.0
                )
                nc.gpsimd.tensor_tensor(
                    out=o[:, bs, :], in0=th1[:], in1=whts[j][:].unsqueeze(1).to_broadcast([P, 4, P]), op=ALU.mult
                )
            else:
                nc.vector.scalar_tensor_tensor(
                    out=o[:, bs, :],
                    in0=thts[(j, c)][:].rearrange("p (b h) -> p b h", b=4),
                    scalar=1.0,
                    in1=whts[j][:].unsqueeze(1).to_broadcast([P, 4, P]),
                    op0=ALU.add,
                    op1=ALU.mult,
                )
            nc.sync.dma_start(out=out_view[:, bs, j * P : (j + 1) * P], in_=o[:, bs, :])

        pos = [0, 0]

        def w_next(k=1):
            for i in range(k):
                if pos[0] < len(w_units):
                    w_turn(*w_units[pos[0]])
                    pos[0] = pos[0] + 1

        q_units = [(ws, j) for j in range(NJ) for ws in ("kv", "q")]

        def w_quant_turned(limit=99):
            for i in range(pos[1], min(len(q_units), pos[1] + limit)):
                ws, j = q_units[i]
                if pos[0] > 3 * j + (1 if ws == "kv" else 2):
                    w_quant(ws, j)
                    pos[1] = i + 1

        def sums(j, c):
            eng = nc.vector if j >= VSUM_FROM else nc.gpsimd
            t1(j, c, eng)
            if c == 1:
                t2(j, c, eng)

        widen(0)
        widen(1)
        w_next(2)
        x_turn(0, 0)
        x_turn(0, 1)
        widen(2)
        widen(3)
        w_next()
        x_turn(1, 0)
        x_turn(1, 1)
        bias_columns()
        w_next(2)
        w_quant_turned(2)
        x_quant(0, 0)
        x_quant(1, 0)
        w_quant_turned()
        w_next()
        for n in range(NJ + LAG):
            a = n
            b = n - LAG
            r = b - 1
            early = b == NJ - 2
            final = b == NJ - 1
            if a < NJ:
                kproj(a, 0)
                qproj(a, 0)
                vproj(a, 0)
            w_quant_turned()
            w_next(3)
            if 0 <= b < NJ and not final:
                kproj(b, 1)
                qproj(b, 1)
                vproj(b, 1)
            if early:
                kproj(b + 1, 1)
                vproj(b + 1, 1)
            if final:
                qproj(b, 1)
            if n < 2:
                widen(4 + 2 * n)
                widen(5 + 2 * n)
            if a < NJ:
                ev(a, 0)
                sums(a, 0)
            for unit in w_units[pos[0] : pos[0] + 3]:
                if unit[1] >= SORT_FROM:
                    w_sort(*unit)
            if 0 <= b < NJ and not final:
                ev(b, 1)
                if b < TSUM_FROM:
                    sums(b, 1)
            if early:
                ev(b + 1, 1)
            if 0 <= r < NJ:
                back_sums(r)
                recip(r)
                whmul(r)
            if n < 2:
                x_turn(2 + n, 0)
                x_turn(2 + n, 1)
            if 0 <= r < NJ:
                back_th(r, 0)
                back_th(r, 1)
            if n < 2:
                w_quant_turned()
            if n == 1:
                x_quant(0, 1)
                x_quant(1, 1)
            if 0 <= r < NJ:
                fin(r, 0)
                fin(r, 1)
            if final:
                back_sums(b)
                recip(b)
                whmul(b)
                back_th(b, 0)
                back_th(b, 1)
                fin(b, 0)
                fin(b, 1)
